import numpy as np
import ml_dtypes


def mxq(x, axis, fmt="e4m3"):
    dtype, down = {"e4m3": (ml_dtypes.float8_e4m3fn, 7), "e5m2": (ml_dtypes.float8_e5m2, 14)}[fmt]
    v = np.moveaxis(np.asarray(x, np.float32).astype(ml_dtypes.bfloat16).astype(np.float64), axis, -1)
    blocks = v.reshape(v.shape[:-1] + (-1, 32))
    amax = np.abs(blocks).max(-1, keepdims=True)
    byte = np.maximum(np.where(amax > 0, np.frexp(amax)[1] - 1 + 127, 0) - down, 1)
    scale = np.exp2(byte - 127.0)
    codes = (blocks / scale).astype(np.float32).astype(dtype).astype(np.float64)
    return np.moveaxis((codes * scale).reshape(v.shape), -1, axis)


WIDE = False


def mx_kscale(k):
    if not WIDE:
        return np.ones(k)
    levels = np.array([10, -10, 5, -5, 0])
    a = np.random.permutation(np.resize(levels, k // 512 * 4)).reshape(k // 512, 4)
    idx = np.arange(k)
    return np.exp2(a[idx // 512, idx % 128 // 32])


BF16 = ml_dtypes.bfloat16


def bf(x):
    return np.asarray(x, np.float32).astype(BF16)


def f64(x):
    return np.asarray(x).astype(np.float64)


N, D, C, M = 12288, 512, 16, 16


def setup_inputs():
    s = mx_kscale(D)
    return {"x": bf(np.random.standard_normal((N, D)) * s),
            "x_var": bf(0.1 + 4.0 * np.random.standard_normal((N, D)) ** 2),
            "prototypes": bf(np.random.standard_normal((C, M, D)) * 0.5 / np.sqrt(D) / s),
            "proto_var": bf(0.1 + 4.0 * np.random.standard_normal((C, M, D)) ** 2)}


def reference(x, x_var, prototypes, proto_var):
    x, x_var, prototypes, proto_var = f64(x), f64(x_var), f64(prototypes), f64(proto_var)
    lamda = 1.0 / x.shape[-1]
    dot = (mxq(x, 1, "e4m3") @ mxq(prototypes.reshape(C * M, D), 1, "e4m3").T).reshape(N, C, M)
    cross = (mxq(np.sqrt(x_var), 1, "e4m3") @ mxq(np.sqrt(proto_var).reshape(C * M, D), 1, "e4m3").T).reshape(N, C, M)
    w2 = (2.0 - 2.0 * dot
          + lamda * (np.sum(x_var, axis=-1)[:, None, None]
                     + np.sum(proto_var, axis=-1)[None, :, :]
                     - 2.0 * cross))
    return -w2

@@ -1,0 +1,231 @@
+from contextlib import ExitStack
+
+import concourse.mybir as mybir
+from concourse.masks import make_identity
+
+F32 = mybir.dt.float32
+BF16 = mybir.dt.bfloat16
+U32 = mybir.dt.uint32
+U8 = mybir.dt.uint8
+FP8X4 = mybir.dt.float8_e4m3fn_x4
+ALU = mybir.AluOpType
+ACT = mybir.ActivationFunctionType
+
+P = 128
+D = 512
+N_ROWS = 12288
+CM = 256
+LAMDA = 1.0 / D
+FLOPS = 2 * 2 * N_ROWS * D * CM
+
+CHUNK_TILES = [2, 2, 4] + [8] * 10 + [4, 2, 2]
+PREFETCH = 5
+PINNED = True
+S_SUM_EVERY = 0
+
+
+def tile_probprotoseghead_t_kernel(tc, x, x_var, prototypes, proto_var, out):
+    nc = tc.nc
+    out2 = out.rearrange("n c m -> n (c m)")
+    p2 = prototypes.rearrange("c m d -> (c m) d")
+    pv2 = proto_var.rearrange("c m d -> (c m) d")
+
+    chunks = []
+    row0 = 0
+    for tiles in CHUNK_TILES:
+        chunks.append((row0, tiles))
+        row0 += tiles * P
+    assert row0 == N_ROWS
+    pairs = []
+    for c, (r0, tiles) in enumerate(chunks):
+        for t0 in range(0, tiles, 2):
+            pairs.append((c, t0))
+    n_pairs = len(pairs)
+    n_chunks = len(chunks)
+
+    with ExitStack() as ctx:
+        consts = ctx.enter_context(tc.tile_pool(name="consts", bufs=1))
+        loads = ctx.enter_context(tc.tile_pool(name="loads", bufs=PREFETCH + 1))
+        stores = ctx.enter_context(tc.tile_pool(name="stores", bufs=6))
+        groups = ctx.enter_context(tc.tile_pool(name="groups", bufs=4))
+        quants = ctx.enter_context(tc.tile_pool(name="quants", bufs=3))
+        small = ctx.enter_context(tc.tile_pool(name="small", bufs=6))
+        junks = ctx.enter_context(tc.tile_pool(name="junks", bufs=2))
+        psum_t = ctx.enter_context(tc.psum_pool(name="psum_t", bufs=3))
+        psum_a = ctx.enter_context(tc.psum_pool(name="psum_a", bufs=2))
+
+        x_tiles = {}
+        v_tiles = {}
+        bn_tiles = {}
+        bs_tiles = {}
+        o_tiles = {}
+        banks = {}
+        g_tiles = {}
+        q_tiles = {}
+        acc_tiles = {}
+
+        def load(c):
+            r0, tiles = chunks[c]
+            x_sb = loads.tile([P, tiles * D], BF16, tag="x")
+            v_sb = loads.tile([P, tiles * D], BF16, tag="v")
+            nc.sync.dma_start(out=x_sb[:], in_=x[r0:r0 + tiles * P, :].rearrange("(p t) d -> p (t d)", t=tiles))
+            nc.sync.dma_start(out=v_sb[:], in_=x_var[r0:r0 + tiles * P, :].rearrange("(p t) d -> p (t d)", t=tiles))
+            x_tiles[c] = x_sb
+            v_tiles[c] = v_sb
+
+        def transpose_pair(bank, words, col0):
+            for u in range(2):
+                for tt in range(2):
+                    nc.tensor.transpose(
+                        bank[:, u * 256 + tt * P:u * 256 + (tt + 1) * P],
+                        words[:, col0 + tt * 256 + u * P:col0 + tt * 256 + (u + 1) * P],
+                        ident[:],
+                    )
+
+        def bf16_pairs(bank):
+            return bank[:].bitcast(BF16).rearrange("q (u n e) -> q n u e", u=2, e=2)
+
+        def grouped_pairs(g, half):
+            return g[:, half * 1024:(half + 1) * 1024].rearrange("q (n u e) -> q n u e", u=2, e=2)
+
+        ident = consts.tile([P, P], F32)
+        make_identity(nc, ident[:])
+        ones = consts.tile([P, P], F32)
+        nc.vector.memset(ones[:], 1.0)
+        if PINNED:
+            ctx.enter_context(tc.manual_schedule())
+        warm = consts.tile([P, 1], F32)
+        nc.scalar.activation(out=warm[:], in_=ones[:, 0:1], func=ACT.Sqrt)
+
+        p_sb = consts.tile([P, 2 * D], BF16)
+        pv_sb = consts.tile([P, 2 * D], BF16)
+        nc.sync.dma_start(out=p_sb[:].rearrange("p (h d) -> p h d", h=2), in_=p2.rearrange("(h p) d -> p h d", p=P))
+        nc.sync.dma_start(out=pv_sb[:].rearrange("p (h d) -> p h d", h=2), in_=pv2.rearrange("(h p) d -> p h d", p=P))
+        for c in range(PREFETCH):
+            load(c)
+
+        tp = psum_t.tile([P, 512], F32, tag="tx")
+        tpv = psum_t.tile([P, 512], F32, tag="tv")
+        transpose_pair(tp, p_sb[:].bitcast(F32), 0)
+        transpose_pair(tpv, pv_sb[:].bitcast(F32), 0)
+        pg = consts.tile([P, 2048], BF16, align_bytes=64)
+        nc.vector.tensor_scalar(out=grouped_pairs(pg, 0), in0=bf16_pairs(tp), scalar1=2.0, scalar2=None, op0=ALU.mult)
+        nc.scalar.activation(out=grouped_pairs(pg, 1), in_=bf16_pairs(tpv), func=ACT.Sqrt, scale=2.0 ** -16)
+        spn = consts.tile([P, 2], F32)
+        rep = consts.tile([P, 2 * P], F32)
+        for h in range(2):
+            junk = junks.tile([P, D], BF16, tag="junkv")
+            nc.vector.tensor_scalar(out=junk[:], in0=pv_sb[:, h * D:(h + 1) * D], scalar1=-LAMDA, scalar2=None,
+                                    op0=ALU.mult, op1=ALU.add, accum_out=spn[:, h:h + 1])
+        for h in range(2):
+            nc.vector.tensor_scalar(out=rep[:, h * P:(h + 1) * P], in0=ones[:], scalar1=spn[:, h:h + 1], scalar2=-2.0,
+                                    op0=ALU.mult, op1=ALU.add)
+        pcodes = consts.tile([P, 512], U32, align_bytes=64)
+        pscl = consts.tile([P, 512], U8, align_bytes=64)
+        nc.vector.quantize_mx(out=pcodes[:].bitcast(FP8X4), scales=pscl[:], in_=pg[:])
+
+        bcm = consts.tile([P, CM], F32)
+
+        def spread_prototype_sums():
+            bb = psum_a.tile([P, CM], F32, tag="acc")
+            for h in range(2):
+                nc.tensor.transpose(bb[:, h * P:(h + 1) * P], rep[:, h * P:(h + 1) * P], ident[:])
+            nc.vector.tensor_copy(out=bcm[:], in_=bb[:])
+
+        def sums(k):
+            c, t0 = pairs[k]
+            tiles = chunks[c][1]
+            if t0 == 0:
+                bn = small.tile([P, tiles], F32, tag="bn")
+                bn_tiles[c] = bn
+            for tt in range(2):
+                t = t0 + tt
+                src = v_tiles[c][:, t * D:(t + 1) * D]
+                if on_scalar(k, tt):
+                    if c not in bs_tiles:
+                        bs = small.tile([P, tiles], F32, tag="bs")
+                        bs_tiles[c] = bs
+                    junk_s = junks.tile([P, D], BF16, tag="junks")
+                    nc.scalar.activation(out=junk_s[:], in_=src, func=ACT.Copy, scale=-LAMDA,
+                                         accum_out=bs_tiles[c][:, t:t + 1])
+                else:
+                    junk_v = junks.tile([P, D], BF16, tag="junkv")
+                    nc.vector.tensor_scalar(out=junk_v[:], in0=src, scalar1=-LAMDA, scalar2=None,
+                                            op0=ALU.mult, op1=ALU.add, accum_out=bn_tiles[c][:, t:t + 1])
+
+        def on_scalar(k, tt):
+            return S_SUM_EVERY > 0 and tt == 1 and k % S_SUM_EVERY == 0
+
+        def transposes(k):
+            c, t0 = pairs[k]
+            tx = psum_t.tile([P, 512], F32, tag="tx")
+            tv = psum_t.tile([P, 512], F32, tag="tv")
+            transpose_pair(tx, x_tiles[c][:].bitcast(F32), t0 * 256)
+            transpose_pair(tv, v_tiles[c][:].bitcast(F32), t0 * 256)
+            banks[k] = (tx, tv)
+
+        def evacuate(k):
+            tx, tv = banks[k]
+            g = groups.tile([P, 2048], BF16, tag="g", align_bytes=64)
+            nc.scalar.copy(out=g[:, 0:1024].bitcast(F32).rearrange("q (n u) -> q n u", u=2),
+                           in_=tx[:].rearrange("q (u n) -> q n u", u=2))
+            nc.scalar.activation(out=grouped_pairs(g, 1), in_=bf16_pairs(tv), func=ACT.Sqrt)
+            g_tiles[k] = g
+
+        def quantise(k):
+            codes = quants.tile([P, 512], U32, tag="codes", align_bytes=64)
+            scl = quants.tile([P, 512], U8, tag="scl", align_bytes=64)
+            nc.vector.quantize_mx(out=codes[:].bitcast(FP8X4), scales=scl[:], in_=g_tiles[k][:])
+            q_tiles[k] = (codes, scl)
+
+        def multiply(k):
+            codes, scl = q_tiles[k]
+            acc = psum_a.tile([P, 2 * CM], F32, tag="acc")
+            for tt in range(2):
+                for half in range(2):
+                    cols = slice(half * 256 + tt * P, half * 256 + (tt + 1) * P)
+                    pcols = slice(half * CM, (half + 1) * CM)
+                    nc.tensor.matmul_mx(
+                        out=acc[:, tt * CM:(tt + 1) * CM],
+                        lhsT=codes[:, cols].bitcast(FP8X4),
+                        lhsT_scale=scl[:, cols],
+                        rhs=pcodes[:, pcols].bitcast(FP8X4),
+                        rhs_scale=pscl[:, pcols],
+                        start=(half == 0),
+                        stop=(half == 1),
+                    )
+            acc_tiles[k] = acc
+
+        def finish(k):
+            c, t0 = pairs[k]
+            r0, tiles = chunks[c]
+            if t0 == 0:
+                o_sb = stores.tile([P, tiles * CM], F32, tag="o")
+                o_tiles[c] = o_sb
+            acc = acc_tiles[k]
+            for tt in range(2):
+                t = t0 + tt
+                b = bs_tiles[c] if on_scalar(k, tt) else bn_tiles[c]
+                nc.vector.scalar_tensor_tensor(
+                    out=o_tiles[c][:, t * CM:(t + 1) * CM], in0=acc[:, tt * CM:(tt + 1) * CM],
+                    scalar=b[:, t:t + 1], in1=bcm[:], op0=ALU.add, op1=ALU.add)
+            if t0 + 2 == tiles:
+                queue = nc.sync if c + PREFETCH >= n_chunks else nc.gpsimd
+                queue.dma_start(out=out2[r0:r0 + tiles * P, :].rearrange("(p t) m -> p (t m)", t=tiles),
+                                in_=o_tiles[c][:])
+
+        for s in range(n_pairs + 3):
+            if s < n_pairs:
+                c, t0 = pairs[s]
+                if t0 == 0 and c + PREFETCH < n_chunks:
+                    load(c + PREFETCH)
+                sums(s)
+                transposes(s)
+                evacuate(s)
+            if s == 1:
+                spread_prototype_sums()
+            if 0 <= s - 2 < n_pairs:
+                quantise(s - 2)
+                multiply(s - 2)
+            if 0 <= s - 3 < n_pairs:
+                finish(s - 3)

@@ -21,7 +21,7 @@ FLOPS = 2 * 2 * N_ROWS * D * CM
 CHUNK_TILES = [2, 2, 4] + [8] * 10 + [4, 2, 2]
 PREFETCH = 5
 PINNED = True
-S_SUM_EVERY = 0
+S_SUM_EVERY = 2
 
 
 def tile_probprotoseghead_t_kernel(tc, x, x_var, prototypes, proto_var, out):

@@ -9,6 +9,7 @@ U32 = mybir.dt.uint32
 U8 = mybir.dt.uint8
 FP8X4 = mybir.dt.float8_e4m3fn_x4
 ALU = mybir.AluOpType
+AX = mybir.AxisListType
 ACT = mybir.ActivationFunctionType
 
 P = 128
@@ -21,7 +22,20 @@ FLOPS = 2 * 2 * N_ROWS * D * CM
 CHUNK_TILES = [2, 2, 4] + [8] * 10 + [4, 2, 2]
 PREFETCH = 5
 PINNED = True
-S_SUM_EVERY = 2
+LOOK = 3
+FOLD_N = 64
+
+
+def sum_route(k, tt):
+    if tt == 0 and k % 5 != 4 and k != 47:
+        return "pe"
+    if tt == 1 and k % 12 == 6:
+        return "s"
+    return "v"
+
+
+def copy_on_vector(k):
+    return False
 
 
 def tile_probprotoseghead_t_kernel(tc, x, x_var, prototypes, proto_var, out):
@@ -49,10 +63,12 @@ def tile_probprotoseghead_t_kernel(tc, x, x_var, prototypes, proto_var, out):
         stores = ctx.enter_context(tc.tile_pool(name="stores", bufs=6))
         groups = ctx.enter_context(tc.tile_pool(name="groups", bufs=4))
         quants = ctx.enter_context(tc.tile_pool(name="quants", bufs=3))
-        small = ctx.enter_context(tc.tile_pool(name="small", bufs=6))
+        small = ctx.enter_context(tc.tile_pool(name="small", bufs=8))
         junks = ctx.enter_context(tc.tile_pool(name="junks", bufs=2))
-        psum_t = ctx.enter_context(tc.psum_pool(name="psum_t", bufs=3))
+        psum_x = ctx.enter_context(tc.psum_pool(name="psum_x", bufs=2))
+        psum_v = ctx.enter_context(tc.psum_pool(name="psum_v", bufs=3))
         psum_a = ctx.enter_context(tc.psum_pool(name="psum_a", bufs=2))
+        psum_f = ctx.enter_context(tc.psum_pool(name="psum_f", bufs=1))
 
         x_tiles = {}
         v_tiles = {}
@@ -63,13 +79,23 @@ def tile_probprotoseghead_t_kernel(tc, x, x_var, prototypes, proto_var, out):
         g_tiles = {}
         q_tiles = {}
         acc_tiles = {}
+        fold_tiles = {}
+
+        ident = consts.tile([P, P], F32)
+        make_identity(nc, ident[:])
+        ones = consts.tile([P, P], F32)
+        nc.vector.memset(ones[:], 1.0)
+        negl = consts.tile([P, P], BF16)
+        nc.vector.tensor_scalar(out=negl[:], in0=ident[:], scalar1=-LAMDA, scalar2=None, op0=ALU.mult)
+        if PINNED:
+            ctx.enter_context(tc.manual_schedule())
 
         def load(c):
             r0, tiles = chunks[c]
             x_sb = loads.tile([P, tiles * D], BF16, tag="x")
             v_sb = loads.tile([P, tiles * D], BF16, tag="v")
-            nc.sync.dma_start(out=x_sb[:], in_=x[r0:r0 + tiles * P, :].rearrange("(p t) d -> p (t d)", t=tiles))
             nc.sync.dma_start(out=v_sb[:], in_=x_var[r0:r0 + tiles * P, :].rearrange("(p t) d -> p (t d)", t=tiles))
+            nc.sync.dma_start(out=x_sb[:], in_=x[r0:r0 + tiles * P, :].rearrange("(p t) d -> p (t d)", t=tiles))
             x_tiles[c] = x_sb
             v_tiles[c] = v_sb
 
@@ -88,87 +114,66 @@ def tile_probprotoseghead_t_kernel(tc, x, x_var, prototypes, proto_var, out):
         def grouped_pairs(g, half):
             return g[:, half * 1024:(half + 1) * 1024].rearrange("q (n u e) -> q n u e", u=2, e=2)
 
-        ident = consts.tile([P, P], F32)
-        make_identity(nc, ident[:])
-        ones = consts.tile([P, P], F32)
-        nc.vector.memset(ones[:], 1.0)
-        if PINNED:
-            ctx.enter_context(tc.manual_schedule())
-        warm = consts.tile([P, 1], F32)
-        nc.scalar.activation(out=warm[:], in_=ones[:, 0:1], func=ACT.Sqrt)
-
-        p_sb = consts.tile([P, 2 * D], BF16)
-        pv_sb = consts.tile([P, 2 * D], BF16)
-        nc.sync.dma_start(out=p_sb[:].rearrange("p (h d) -> p h d", h=2), in_=p2.rearrange("(h p) d -> p h d", p=P))
-        nc.sync.dma_start(out=pv_sb[:].rearrange("p (h d) -> p h d", h=2), in_=pv2.rearrange("(h p) d -> p h d", p=P))
-        for c in range(PREFETCH):
-            load(c)
-
-        tp = psum_t.tile([P, 512], F32, tag="tx")
-        tpv = psum_t.tile([P, 512], F32, tag="tv")
-        transpose_pair(tp, p_sb[:].bitcast(F32), 0)
-        transpose_pair(tpv, pv_sb[:].bitcast(F32), 0)
-        pg = consts.tile([P, 2048], BF16, align_bytes=64)
-        nc.vector.tensor_scalar(out=grouped_pairs(pg, 0), in0=bf16_pairs(tp), scalar1=2.0, scalar2=None, op0=ALU.mult)
-        nc.scalar.activation(out=grouped_pairs(pg, 1), in_=bf16_pairs(tpv), func=ACT.Sqrt, scale=2.0 ** -16)
-        spn = consts.tile([P, 2], F32)
-        rep = consts.tile([P, 2 * P], F32)
-        for h in range(2):
-            junk = junks.tile([P, D], BF16, tag="junkv")
-            nc.vector.tensor_scalar(out=junk[:], in0=pv_sb[:, h * D:(h + 1) * D], scalar1=-LAMDA, scalar2=None,
-                                    op0=ALU.mult, op1=ALU.add, accum_out=spn[:, h:h + 1])
-        for h in range(2):
-            nc.vector.tensor_scalar(out=rep[:, h * P:(h + 1) * P], in0=ones[:], scalar1=spn[:, h:h + 1], scalar2=-2.0,
-                                    op0=ALU.mult, op1=ALU.add)
-        pcodes = consts.tile([P, 512], U32, align_bytes=64)
-        pscl = consts.tile([P, 512], U8, align_bytes=64)
-        nc.vector.quantize_mx(out=pcodes[:].bitcast(FP8X4), scales=pscl[:], in_=pg[:])
-
-        bcm = consts.tile([P, CM], F32)
-
-        def spread_prototype_sums():
-            bb = psum_a.tile([P, CM], F32, tag="acc")
-            for h in range(2):
-                nc.tensor.transpose(bb[:, h * P:(h + 1) * P], rep[:, h * P:(h + 1) * P], ident[:])
-            nc.vector.tensor_copy(out=bcm[:], in_=bb[:])
+        def bias_tile(c, route):
+            table = bs_tiles if route == "s" else bn_tiles
+            if c not in table:
+                b = small.tile([P, chunks[c][1]], F32, tag="bs" if route == "s" else "bn")
+                table[c] = b
+            return table[c]
 
         def sums(k):
             c, t0 = pairs[k]
-            tiles = chunks[c][1]
-            if t0 == 0:
-                bn = small.tile([P, tiles], F32, tag="bn")
-                bn_tiles[c] = bn
             for tt in range(2):
                 t = t0 + tt
+                route = sum_route(k, tt)
                 src = v_tiles[c][:, t * D:(t + 1) * D]
-                if on_scalar(k, tt):
-                    if c not in bs_tiles:
-                        bs = small.tile([P, tiles], F32, tag="bs")
-                        bs_tiles[c] = bs
+                if route == "s":
                     junk_s = junks.tile([P, D], BF16, tag="junks")
                     nc.scalar.activation(out=junk_s[:], in_=src, func=ACT.Copy, scale=-LAMDA,
-                                         accum_out=bs_tiles[c][:, t:t + 1])
-                else:
+                                         accum_out=bias_tile(c, route)[:, t:t + 1])
+                elif route == "v":
                     junk_v = junks.tile([P, D], BF16, tag="junkv")
                     nc.vector.tensor_scalar(out=junk_v[:], in0=src, scalar1=-LAMDA, scalar2=None,
-                                            op0=ALU.mult, op1=ALU.add, accum_out=bn_tiles[c][:, t:t + 1])
+                                            op0=ALU.mult, op1=ALU.add, accum_out=bias_tile(c, route)[:, t:t + 1])
 
-        def on_scalar(k, tt):
-            return S_SUM_EVERY > 0 and tt == 1 and k % S_SUM_EVERY == 0
+        def fold(k):
+            c, t0 = pairs[k]
+            for tt in range(2):
+                if sum_route(k, tt) == "pe":
+                    t = t0 + tt
+                    ft = psum_f.tile([P, FOLD_N], F32, tag="fold")
+                    n_folds = D // FOLD_N
+                    for j in range(n_folds):
+                        nc.tensor.matmul(out=ft[:], lhsT=negl[:],
+                                         rhs=v_tiles[c][:, t * D + j * FOLD_N:t * D + (j + 1) * FOLD_N],
+                                         start=(j == 0), stop=(j == n_folds - 1))
+                    fold_tiles[(k, tt)] = ft
+
+        def fold_reduce(k):
+            c, t0 = pairs[k]
+            for tt in range(2):
+                if sum_route(k, tt) == "pe":
+                    t = t0 + tt
+                    nc.vector.tensor_reduce(out=bias_tile(c, "pe")[:, t:t + 1], in_=fold_tiles[(k, tt)][:],
+                                            axis=AX.X, op=ALU.add)
 
         def transposes(k):
             c, t0 = pairs[k]
-            tx = psum_t.tile([P, 512], F32, tag="tx")
-            tv = psum_t.tile([P, 512], F32, tag="tv")
-            transpose_pair(tx, x_tiles[c][:].bitcast(F32), t0 * 256)
+            tv = psum_v.tile([P, 512], F32, tag="tv")
             transpose_pair(tv, v_tiles[c][:].bitcast(F32), t0 * 256)
+            tx = psum_x.tile([P, 512], F32, tag="tx")
+            transpose_pair(tx, x_tiles[c][:].bitcast(F32), t0 * 256)
             banks[k] = (tx, tv)
 
         def evacuate(k):
             tx, tv = banks[k]
             g = groups.tile([P, 2048], BF16, tag="g", align_bytes=64)
-            nc.scalar.copy(out=g[:, 0:1024].bitcast(F32).rearrange("q (n u) -> q n u", u=2),
-                           in_=tx[:].rearrange("q (u n) -> q n u", u=2))
+            x_out = g[:, 0:1024].bitcast(F32).rearrange("q (n u) -> q n u", u=2)
+            x_in = tx[:].rearrange("q (u n) -> q n u", u=2)
+            if copy_on_vector(k):
+                nc.vector.tensor_copy(out=x_out, in_=x_in)
+            else:
+                nc.scalar.copy(out=x_out, in_=x_in)
             nc.scalar.activation(out=grouped_pairs(g, 1), in_=bf16_pairs(tv), func=ACT.Sqrt)
             g_tiles[k] = g
 
@@ -205,7 +210,7 @@ def tile_probprotoseghead_t_kernel(tc, x, x_var, prototypes, proto_var, out):
             acc = acc_tiles[k]
             for tt in range(2):
                 t = t0 + tt
-                b = bs_tiles[c] if on_scalar(k, tt) else bn_tiles[c]
+                b = bias_tile(c, sum_route(k, tt))
                 nc.vector.scalar_tensor_tensor(
                     out=o_tiles[c][:, t * CM:(t + 1) * CM], in0=acc[:, tt * CM:(tt + 1) * CM],
                     scalar=b[:, t:t + 1], in1=bcm[:], op0=ALU.add, op1=ALU.add)
@@ -214,13 +219,58 @@ def tile_probprotoseghead_t_kernel(tc, x, x_var, prototypes, proto_var, out):
                 queue.dma_start(out=out2[r0:r0 + tiles * P, :].rearrange("(p t) m -> p (t m)", t=tiles),
                                 in_=o_tiles[c][:])
 
+        warm = consts.tile([P, 1], F32)
+        nc.scalar.activation(out=warm[:], in_=ones[:, 0:1], func=ACT.Sqrt)
+        p_sb = consts.tile([P, 2 * D], BF16)
+        pv_sb = consts.tile([P, 2 * D], BF16)
+        nc.sync.dma_start(out=pv_sb[:].rearrange("p (h d) -> p h d", h=2), in_=pv2.rearrange("(h p) d -> p h d", p=P))
+        nc.sync.dma_start(out=p_sb[:].rearrange("p (h d) -> p h d", h=2), in_=p2.rearrange("(h p) d -> p h d", p=P))
+        for c in range(PREFETCH):
+            load(c)
+
+        tpv = psum_v.tile([P, 512], F32, tag="tv")
+        transpose_pair(tpv, pv_sb[:].bitcast(F32), 0)
+        tp = psum_x.tile([P, 512], F32, tag="tx")
+        transpose_pair(tp, p_sb[:].bitcast(F32), 0)
+        pg = consts.tile([P, 2048], BF16, align_bytes=64)
+        nc.scalar.activation(out=grouped_pairs(pg, 1), in_=bf16_pairs(tpv), func=ACT.Sqrt, scale=2.0 ** -16)
+        spn = consts.tile([P, 2], F32)
+        rep = consts.tile([P, 2 * P], F32)
+        for h in range(2):
+            junk = junks.tile([P, D], BF16, tag="junkv")
+            nc.vector.tensor_scalar(out=junk[:], in0=pv_sb[:, h * D:(h + 1) * D], scalar1=-LAMDA, scalar2=None,
+                                    op0=ALU.mult, op1=ALU.add, accum_out=spn[:, h:h + 1])
+        for h in range(2):
+            nc.vector.tensor_scalar(out=rep[:, h * P:(h + 1) * P], in0=ones[:], scalar1=spn[:, h:h + 1], scalar2=-2.0,
+                                    op0=ALU.mult, op1=ALU.add)
+        nc.vector.tensor_scalar(out=grouped_pairs(pg, 0), in0=bf16_pairs(tp), scalar1=2.0, scalar2=None, op0=ALU.mult)
+        for k in range(min(2, LOOK)):
+            sums(k)
+        pcodes = consts.tile([P, 512], U32, align_bytes=64)
+        pscl = consts.tile([P, 512], U8, align_bytes=64)
+        nc.vector.quantize_mx(out=pcodes[:].bitcast(FP8X4), scales=pscl[:], in_=pg[:])
+        for k in range(min(2, LOOK), LOOK):
+            sums(k)
+        bcm = consts.tile([P, CM], F32)
+
+        def spread_prototype_sums():
+            bb = psum_a.tile([P, CM], F32, tag="acc")
+            for h in range(2):
+                nc.tensor.transpose(bb[:, h * P:(h + 1) * P], rep[:, h * P:(h + 1) * P], ident[:])
+            nc.vector.tensor_copy(out=bcm[:], in_=bb[:])
+
+        fold(0)
         for s in range(n_pairs + 3):
             if s < n_pairs:
                 c, t0 = pairs[s]
                 if t0 == 0 and c + PREFETCH < n_chunks:
                     load(c + PREFETCH)
-                sums(s)
+                fold_reduce(s)
+                if s + LOOK < n_pairs:
+                    sums(s + LOOK)
                 transposes(s)
+                if s + 1 < n_pairs:
+                    fold(s + 1)
                 evacuate(s)
             if s == 1:
                 spread_prototype_sums()

@@ -19,10 +19,10 @@ CM = 256
 LAMDA = 1.0 / D
 FLOPS = 2 * 2 * N_ROWS * D * CM
 
-CHUNK_TILES = [2, 2, 4] + [8] * 10 + [4, 2, 2]
+CHUNK_TILES = [2, 2, 4, 4] + [8] * 9 + [4, 4, 2, 2]
 PREFETCH = 5
 PINNED = True
-LOOK = 3
+LOOK = 4
 FOLD_N = 64
 
 
@@ -62,13 +62,13 @@ def tile_probprotoseghead_t_kernel(tc, x, x_var, prototypes, proto_var, out):
         loads = ctx.enter_context(tc.tile_pool(name="loads", bufs=PREFETCH + 1))
         stores = ctx.enter_context(tc.tile_pool(name="stores", bufs=6))
         groups = ctx.enter_context(tc.tile_pool(name="groups", bufs=4))
-        quants = ctx.enter_context(tc.tile_pool(name="quants", bufs=3))
+        quants = ctx.enter_context(tc.tile_pool(name="quants", bufs=4))
         small = ctx.enter_context(tc.tile_pool(name="small", bufs=8))
         junks = ctx.enter_context(tc.tile_pool(name="junks", bufs=2))
         psum_x = ctx.enter_context(tc.psum_pool(name="psum_x", bufs=2))
-        psum_v = ctx.enter_context(tc.psum_pool(name="psum_v", bufs=3))
+        psum_v = ctx.enter_context(tc.psum_pool(name="psum_v", bufs=2))
         psum_a = ctx.enter_context(tc.psum_pool(name="psum_a", bufs=2))
-        psum_f = ctx.enter_context(tc.psum_pool(name="psum_f", bufs=1))
+        psum_f = ctx.enter_context(tc.psum_pool(name="psum_f", bufs=2))
 
         x_tiles = {}
         v_tiles = {}
@@ -170,11 +170,11 @@ def tile_probprotoseghead_t_kernel(tc, x, x_var, prototypes, proto_var, out):
             g = groups.tile([P, 2048], BF16, tag="g", align_bytes=64)
             x_out = g[:, 0:1024].bitcast(F32).rearrange("q (n u) -> q n u", u=2)
             x_in = tx[:].rearrange("q (u n) -> q n u", u=2)
+            nc.scalar.activation(out=grouped_pairs(g, 1), in_=bf16_pairs(tv), func=ACT.Sqrt)
             if copy_on_vector(k):
                 nc.vector.tensor_copy(out=x_out, in_=x_in)
             else:
                 nc.scalar.copy(out=x_out, in_=x_in)
-            nc.scalar.activation(out=grouped_pairs(g, 1), in_=bf16_pairs(tv), func=ACT.Sqrt)
             g_tiles[k] = g
 
         def quantise(k):
@@ -259,23 +259,45 @@ def tile_probprotoseghead_t_kernel(tc, x, x_var, prototypes, proto_var, out):
                 nc.tensor.transpose(bb[:, h * P:(h + 1) * P], rep[:, h * P:(h + 1) * P], ident[:])
             nc.vector.tensor_copy(out=bcm[:], in_=bb[:])
 
-        fold(0)
-        for s in range(n_pairs + 3):
-            if s < n_pairs:
-                c, t0 = pairs[s]
-                if t0 == 0 and c + PREFETCH < n_chunks:
-                    load(c + PREFETCH)
-                fold_reduce(s)
-                if s + LOOK < n_pairs:
-                    sums(s + LOOK)
-                transposes(s)
-                if s + 1 < n_pairs:
-                    fold(s + 1)
-                evacuate(s)
-            if s == 1:
+        assert n_pairs % 2 == 0 and LOOK % 2 == 0
+        n_quads = n_pairs // 2
+        for k in range(2):
+            fold(k)
+        for k in range(2):
+            fold_reduce(k)
+        for j in range(n_quads + 1):
+            first, second = 2 * j, 2 * j + 1
+            if j < n_quads:
+                for k in (first, second):
+                    transposes(k)
+                for k in (first, second):
+                    c, t0 = pairs[k]
+                    if t0 == 0 and c + PREFETCH < n_chunks:
+                        load(c + PREFETCH)
+                for k in (first + 2, second + 2):
+                    if k < n_pairs:
+                        fold(k)
+                for k in (first, second):
+                    evacuate(k)
+            if j == 0:
                 spread_prototype_sums()
-            if 0 <= s - 2 < n_pairs:
-                quantise(s - 2)
-                multiply(s - 2)
-            if 0 <= s - 3 < n_pairs:
-                finish(s - 3)
+            if j >= 1:
+                quantise(first - 1)
+                if j < n_quads:
+                    multiply(first - 2)
+                multiply(first - 1)
+            if j == 0:
+                quantise(first)
+            for k in (first + LOOK, second + LOOK):
+                if k < n_pairs:
+                    sums(k)
+            for k in (first + 2, second + 2):
+                if k < n_pairs:
+                    fold_reduce(k)
+            if 0 < j < n_quads:
+                quantise(first)
+            if j >= 1:
+                finish(first - 2)
+                finish(first - 1)
+            if j == n_quads - 1:
+                multiply(first)

@@ -27,9 +27,9 @@ FOLD_N = 64
 
 
 def sum_route(k, tt):
-    if tt == 0 and k % 5 != 4 and k != 47:
+    if tt == 0 and 2 <= k // 2 <= 22 and k // 2 not in (9, 16):
         return "pe"
-    if tt == 1 and k % 12 == 6:
+    if tt == 1 and k % 7 == 6:
         return "s"
     return "v"
 
@@ -66,9 +66,9 @@ def tile_probprotoseghead_t_kernel(tc, x, x_var, prototypes, proto_var, out):
         small = ctx.enter_context(tc.tile_pool(name="small", bufs=8))
         junks = ctx.enter_context(tc.tile_pool(name="junks", bufs=2))
         psum_x = ctx.enter_context(tc.psum_pool(name="psum_x", bufs=2))
-        psum_v = ctx.enter_context(tc.psum_pool(name="psum_v", bufs=2))
+        psum_v = ctx.enter_context(tc.psum_pool(name="psum_v", bufs=3))
         psum_a = ctx.enter_context(tc.psum_pool(name="psum_a", bufs=2))
-        psum_f = ctx.enter_context(tc.psum_pool(name="psum_f", bufs=2))
+        psum_f = ctx.enter_context(tc.psum_pool(name="psum_f", bufs=1))
 
         x_tiles = {}
         v_tiles = {}
@@ -80,6 +80,7 @@ def tile_probprotoseghead_t_kernel(tc, x, x_var, prototypes, proto_var, out):
         q_tiles = {}
         acc_tiles = {}
         fold_tiles = {}
+        bf_tiles = {}
 
         ident = consts.tile([P, P], F32)
         make_identity(nc, ident[:])
@@ -121,6 +122,13 @@ def tile_probprotoseghead_t_kernel(tc, x, x_var, prototypes, proto_var, out):
                 table[c] = b
             return table[c]
 
+        def row_bias(k, tt):
+            route = sum_route(k, tt)
+            if route == "pe":
+                return bf_tiles[k // 2][:, k % 2:k % 2 + 1]
+            c, t0 = pairs[k]
+            return bias_tile(c, route)[:, t0 + tt:t0 + tt + 1]
+
         def sums(k):
             c, t0 = pairs[k]
             for tt in range(2):
@@ -136,37 +144,42 @@ def tile_probprotoseghead_t_kernel(tc, x, x_var, prototypes, proto_var, out):
                     nc.vector.tensor_scalar(out=junk_v[:], in0=src, scalar1=-LAMDA, scalar2=None,
                                             op0=ALU.mult, op1=ALU.add, accum_out=bias_tile(c, route)[:, t:t + 1])
 
-        def fold(k):
-            c, t0 = pairs[k]
-            for tt in range(2):
-                if sum_route(k, tt) == "pe":
-                    t = t0 + tt
-                    ft = psum_f.tile([P, FOLD_N], F32, tag="fold")
-                    n_folds = D // FOLD_N
-                    for j in range(n_folds):
-                        nc.tensor.matmul(out=ft[:], lhsT=negl[:],
-                                         rhs=v_tiles[c][:, t * D + j * FOLD_N:t * D + (j + 1) * FOLD_N],
-                                         start=(j == 0), stop=(j == n_folds - 1))
-                    fold_tiles[(k, tt)] = ft
+        def fold(j):
+            if sum_route(2 * j, 0) != "pe":
+                return
+            ft = psum_f.tile([P, 2 * FOLD_N], F32, tag="fold")
+            n_folds = D // FOLD_N
+            for i in range(2):
+                c, t0 = pairs[2 * j + i]
+                for f in range(n_folds):
+                    nc.tensor.matmul(out=ft[:, i * FOLD_N:(i + 1) * FOLD_N], lhsT=negl[:],
+                                     rhs=v_tiles[c][:, t0 * D + f * FOLD_N:t0 * D + (f + 1) * FOLD_N],
+                                     start=(f == 0), stop=(f == n_folds - 1))
+            fold_tiles[j] = ft
 
-        def fold_reduce(k):
-            c, t0 = pairs[k]
-            for tt in range(2):
-                if sum_route(k, tt) == "pe":
-                    t = t0 + tt
-                    nc.vector.tensor_reduce(out=bias_tile(c, "pe")[:, t:t + 1], in_=fold_tiles[(k, tt)][:],
-                                            axis=AX.X, op=ALU.add)
+        def fold_reduce(j):
+            if sum_route(2 * j, 0) != "pe":
+                return
+            bf = small.tile([P, 2], F32, tag="bf")
+            nc.vector.tensor_reduce(out=bf[:], in_=fold_tiles[j][:].rearrange("p (i n) -> p i n", i=2),
+                                    axis=AX.X, op=ALU.add)
+            bf_tiles[j] = bf
 
-        def transposes(k):
+        def transpose_v(k):
             c, t0 = pairs[k]
             tv = psum_v.tile([P, 512], F32, tag="tv")
             transpose_pair(tv, v_tiles[c][:].bitcast(F32), t0 * 256)
+            banks[("v", k)] = tv
+
+        def transpose_x(k):
+            c, t0 = pairs[k]
             tx = psum_x.tile([P, 512], F32, tag="tx")
             transpose_pair(tx, x_tiles[c][:].bitcast(F32), t0 * 256)
-            banks[k] = (tx, tv)
+            banks[("x", k)] = tx
 
         def evacuate(k):
-            tx, tv = banks[k]
+            tx = banks[("x", k)]
+            tv = banks[("v", k)]
             g = groups.tile([P, 2048], BF16, tag="g", align_bytes=64)
             x_out = g[:, 0:1024].bitcast(F32).rearrange("q (n u) -> q n u", u=2)
             x_in = tx[:].rearrange("q (u n) -> q n u", u=2)
@@ -210,10 +223,9 @@ def tile_probprotoseghead_t_kernel(tc, x, x_var, prototypes, proto_var, out):
             acc = acc_tiles[k]
             for tt in range(2):
                 t = t0 + tt
-                b = bias_tile(c, sum_route(k, tt))
                 nc.vector.scalar_tensor_tensor(
                     out=o_tiles[c][:, t * CM:(t + 1) * CM], in0=acc[:, tt * CM:(tt + 1) * CM],
-                    scalar=b[:, t:t + 1], in1=bcm[:], op0=ALU.add, op1=ALU.add)
+                    scalar=row_bias(k, tt), in1=bcm[:], op0=ALU.add, op1=ALU.add)
             if t0 + 2 == tiles:
                 queue = nc.sync if c + PREFETCH >= n_chunks else nc.gpsimd
                 queue.dma_start(out=out2[r0:r0 + tiles * P, :].rearrange("(p t) m -> p (t m)", t=tiles),
@@ -261,26 +273,25 @@ def tile_probprotoseghead_t_kernel(tc, x, x_var, prototypes, proto_var, out):
 
         assert n_pairs % 2 == 0 and LOOK % 2 == 0
         n_quads = n_pairs // 2
-        for k in range(2):
-            fold(k)
-        for k in range(2):
-            fold_reduce(k)
+        transpose_v(0)
         for j in range(n_quads + 1):
             first, second = 2 * j, 2 * j + 1
             if j < n_quads:
-                for k in (first, second):
-                    transposes(k)
+                transpose_x(first)
+                transpose_v(second)
+                if second + 1 < n_pairs:
+                    transpose_v(second + 1)
+                transpose_x(second)
                 for k in (first, second):
                     c, t0 = pairs[k]
                     if t0 == 0 and c + PREFETCH < n_chunks:
                         load(c + PREFETCH)
-                for k in (first + 2, second + 2):
-                    if k < n_pairs:
-                        fold(k)
+                if j == 0:
+                    spread_prototype_sums()
+                if j + 1 < n_quads:
+                    fold(j + 1)
                 for k in (first, second):
                     evacuate(k)
-            if j == 0:
-                spread_prototype_sums()
             if j >= 1:
                 quantise(first - 1)
                 if j < n_quads:
@@ -291,9 +302,8 @@ def tile_probprotoseghead_t_kernel(tc, x, x_var, prototypes, proto_var, out):
             for k in (first + LOOK, second + LOOK):
                 if k < n_pairs:
                     sums(k)
-            for k in (first + 2, second + 2):
-                if k < n_pairs:
-                    fold_reduce(k)
+            if j + 1 < n_quads:
+                fold_reduce(j + 1)
             if 0 < j < n_quads:
                 quantise(first)
             if j >= 1:

@@ -29,7 +29,7 @@ FOLD_N = 64
 def sum_route(k, tt):
     if tt == 0 and 2 <= k // 2 <= 22 and k // 2 not in (9, 16):
         return "pe"
-    if tt == 1 and k % 7 == 6:
+    if tt == 1 and k % 7 == 6 and k < 40:
         return "s"
     return "v"
 
@@ -177,59 +177,81 @@ def tile_probprotoseghead_t_kernel(tc, x, x_var, prototypes, proto_var, out):
             transpose_pair(tx, x_tiles[c][:].bitcast(F32), t0 * 256)
             banks[("x", k)] = tx
 
-        def evacuate(k):
-            tx = banks[("x", k)]
-            tv = banks[("v", k)]
-            g = groups.tile([P, 2048], BF16, tag="g", align_bytes=64)
-            x_out = g[:, 0:1024].bitcast(F32).rearrange("q (n u) -> q n u", u=2)
-            x_in = tx[:].rearrange("q (u n) -> q n u", u=2)
-            nc.scalar.activation(out=grouped_pairs(g, 1), in_=bf16_pairs(tv), func=ACT.Sqrt)
-            if copy_on_vector(k):
-                nc.vector.tensor_copy(out=x_out, in_=x_in)
-            else:
-                nc.scalar.copy(out=x_out, in_=x_in)
-            g_tiles[k] = g
+        def group_tile(k):
+            if k not in g_tiles:
+                g = groups.tile([P, 2048], BF16, tag="g", align_bytes=64)
+                g_tiles[k] = g
+            return g_tiles[k]
 
-        def quantise(k):
-            codes = quants.tile([P, 512], U32, tag="codes", align_bytes=64)
-            scl = quants.tile([P, 512], U8, tag="scl", align_bytes=64)
-            nc.vector.quantize_mx(out=codes[:].bitcast(FP8X4), scales=scl[:], in_=g_tiles[k][:])
-            q_tiles[k] = (codes, scl)
+        def copy_x(k):
+            nc.scalar.copy(out=group_tile(k)[:, 0:1024].bitcast(F32).rearrange("q (n u) -> q n u", u=2),
+                           in_=banks[("x", k)][:].rearrange("q (u n) -> q n u", u=2))
+
+        def root_v(k, n0, n1):
+            nc.scalar.activation(out=grouped_pairs(group_tile(k), 1)[:, n0:n1], in_=bf16_pairs(banks[("v", k)])[:, n0:n1],
+                                 func=ACT.Sqrt)
+
+        def evacuate(k):
+            root_v(k, 0, 2 * P)
+            copy_x(k)
+
+        def quantise(k, col0=0, col1=2048):
+            if k not in q_tiles:
+                codes = quants.tile([P, 512], U32, tag="codes", align_bytes=64)
+                scl = quants.tile([P, 512], U8, tag="scl", align_bytes=64)
+                q_tiles[k] = (codes, scl)
+            codes, scl = q_tiles[k]
+            nc.vector.quantize_mx(out=codes[:, col0 // 4:col1 // 4].bitcast(FP8X4), scales=scl[:, col0 // 4:col1 // 4],
+                                  in_=g_tiles[k][:, col0:col1])
+
+        def multiply_tile(k, tt):
+            codes, scl = q_tiles[k]
+            if k not in acc_tiles:
+                acc = psum_a.tile([P, 2 * CM], F32, tag="acc")
+                acc_tiles[k] = acc
+            for half in range(2):
+                cols = slice(half * 256 + tt * P, half * 256 + (tt + 1) * P)
+                pcols = slice(half * CM, (half + 1) * CM)
+                nc.tensor.matmul_mx(
+                    out=acc_tiles[k][:, tt * CM:(tt + 1) * CM],
+                    lhsT=codes[:, cols].bitcast(FP8X4),
+                    lhsT_scale=scl[:, cols],
+                    rhs=pcodes[:, pcols].bitcast(FP8X4),
+                    rhs_scale=pscl[:, pcols],
+                    start=(half == 0),
+                    stop=(half == 1),
+                )
 
         def multiply(k):
-            codes, scl = q_tiles[k]
-            acc = psum_a.tile([P, 2 * CM], F32, tag="acc")
             for tt in range(2):
-                for half in range(2):
-                    cols = slice(half * 256 + tt * P, half * 256 + (tt + 1) * P)
-                    pcols = slice(half * CM, (half + 1) * CM)
-                    nc.tensor.matmul_mx(
-                        out=acc[:, tt * CM:(tt + 1) * CM],
-                        lhsT=codes[:, cols].bitcast(FP8X4),
-                        lhsT_scale=scl[:, cols],
-                        rhs=pcodes[:, pcols].bitcast(FP8X4),
-                        rhs_scale=pscl[:, pcols],
-                        start=(half == 0),
-                        stop=(half == 1),
-                    )
-            acc_tiles[k] = acc
+                multiply_tile(k, tt)
+
+        def finish_tile(k, tt):
+            c, t0 = pairs[k]
+            if c not in o_tiles:
+                o_sb = stores.tile([P, chunks[c][1] * CM], F32, tag="o")
+                o_tiles[c] = o_sb
+            t = t0 + tt
+            nc.vector.scalar_tensor_tensor(
+                out=o_tiles[c][:, t * CM:(t + 1) * CM], in0=acc_tiles[k][:, tt * CM:(tt + 1) * CM],
+                scalar=row_bias(k, tt), in1=bcm[:], op0=ALU.add, op1=ALU.add)
 
         def finish(k):
             c, t0 = pairs[k]
             r0, tiles = chunks[c]
-            if t0 == 0:
-                o_sb = stores.tile([P, tiles * CM], F32, tag="o")
-                o_tiles[c] = o_sb
-            acc = acc_tiles[k]
             for tt in range(2):
-                t = t0 + tt
-                nc.vector.scalar_tensor_tensor(
-                    out=o_tiles[c][:, t * CM:(t + 1) * CM], in0=acc[:, tt * CM:(tt + 1) * CM],
-                    scalar=row_bias(k, tt), in1=bcm[:], op0=ALU.add, op1=ALU.add)
+                finish_tile(k, tt)
             if t0 + 2 == tiles:
                 queue = nc.sync if c + PREFETCH >= n_chunks else nc.gpsimd
                 queue.dma_start(out=out2[r0:r0 + tiles * P, :].rearrange("(p t) m -> p (t m)", t=tiles),
                                 in_=o_tiles[c][:])
+
+        def store_tile(k, tt):
+            c, t0 = pairs[k]
+            r0, tiles = chunks[c]
+            t = t0 + tt
+            nc.sync.dma_start(out=out2[r0:r0 + tiles * P, :].rearrange("(p t) m -> p t m", t=tiles)[:, t, :],
+                              in_=o_tiles[c][:, t * CM:(t + 1) * CM])
 
         warm = consts.tile([P, 1], F32)
         nc.scalar.activation(out=warm[:], in_=ones[:, 0:1], func=ACT.Sqrt)
@@ -273,41 +295,52 @@ def tile_probprotoseghead_t_kernel(tc, x, x_var, prototypes, proto_var, out):
 
         assert n_pairs % 2 == 0 and LOOK % 2 == 0
         n_quads = n_pairs // 2
+        last = n_pairs - 1
         transpose_v(0)
-        for j in range(n_quads + 1):
+        for j in range(n_quads):
             first, second = 2 * j, 2 * j + 1
-            if j < n_quads:
-                transpose_x(first)
-                transpose_v(second)
-                if second + 1 < n_pairs:
-                    transpose_v(second + 1)
-                transpose_x(second)
-                for k in (first, second):
-                    c, t0 = pairs[k]
-                    if t0 == 0 and c + PREFETCH < n_chunks:
-                        load(c + PREFETCH)
-                if j == 0:
-                    spread_prototype_sums()
-                if j + 1 < n_quads:
-                    fold(j + 1)
-                for k in (first, second):
-                    evacuate(k)
+            transpose_x(first)
+            transpose_v(second)
+            if second < last:
+                transpose_v(second + 1)
+            transpose_x(second)
+            for k in (first, second):
+                c, t0 = pairs[k]
+                if t0 == 0 and c + PREFETCH < n_chunks:
+                    load(c + PREFETCH)
+            if j == 0:
+                spread_prototype_sums()
+            if j + 1 < n_quads:
+                fold(j + 1)
+            evacuate(first)
+            if second < last:
+                evacuate(second)
+            else:
+                copy_x(last)
+                root_v(last, 0, P)
+                root_v(last, P, 2 * P)
             if j >= 1:
                 quantise(first - 1)
-                if j < n_quads:
-                    multiply(first - 2)
+                multiply(first - 2)
                 multiply(first - 1)
-            if j == 0:
+            else:
                 quantise(first)
             for k in (first + LOOK, second + LOOK):
                 if k < n_pairs:
                     sums(k)
             if j + 1 < n_quads:
                 fold_reduce(j + 1)
-            if 0 < j < n_quads:
-                quantise(first)
             if j >= 1:
+                quantise(first)
                 finish(first - 2)
                 finish(first - 1)
-            if j == n_quads - 1:
-                multiply(first)
+        multiply(last - 1)
+        quantise(last, 0, 1024)
+        quantise(last, 1024, 1536)
+        multiply_tile(last, 0)
+        quantise(last, 1536, 2048)
+        multiply_tile(last, 1)
+        finish(last - 1)
+        for tt in range(2):
+            finish_tile(last, tt)
+            store_tile(last, tt)

@@ -242,7 +242,7 @@ def tile_probprotoseghead_t_kernel(tc, x, x_var, prototypes, proto_var, out):
             for tt in range(2):
                 finish_tile(k, tt)
             if t0 + 2 == tiles:
-                queue = nc.sync if c + PREFETCH >= n_chunks else nc.gpsimd
+                queue = nc.sync
                 queue.dma_start(out=out2[r0:r0 + tiles * P, :].rearrange("(p t) m -> p (t m)", t=tiles),
                                 in_=o_tiles[c][:])
 

@@ -29,13 +29,9 @@ FOLD_N = 64
 def sum_route(k, tt):
     if tt == 0 and 2 <= k // 2 <= 22 and k // 2 not in (9, 16):
         return "pe"
-    if tt == 1 and k % 7 == 6 and k < 40:
-        return "s"
+    if tt == 1 and k % 2 == 1 and k // 2 >= 2:
+        return "g"
     return "v"
-
-
-def copy_on_vector(k):
-    return False
 
 
 def tile_probprotoseghead_t_kernel(tc, x, x_var, prototypes, proto_var, out):
@@ -65,6 +61,7 @@ def tile_probprotoseghead_t_kernel(tc, x, x_var, prototypes, proto_var, out):
         quants = ctx.enter_context(tc.tile_pool(name="quants", bufs=4))
         small = ctx.enter_context(tc.tile_pool(name="small", bufs=8))
         junks = ctx.enter_context(tc.tile_pool(name="junks", bufs=2))
+        pools = ctx.enter_context(tc.tile_pool(name="pools", bufs=2))
         psum_x = ctx.enter_context(tc.psum_pool(name="psum_x", bufs=2))
         psum_v = ctx.enter_context(tc.psum_pool(name="psum_v", bufs=3))
         psum_a = ctx.enter_context(tc.psum_pool(name="psum_a", bufs=2))
@@ -73,7 +70,8 @@ def tile_probprotoseghead_t_kernel(tc, x, x_var, prototypes, proto_var, out):
         x_tiles = {}
         v_tiles = {}
         bn_tiles = {}
-        bs_tiles = {}
+        gs_tiles = {}
+        gb_tiles = {}
         o_tiles = {}
         banks = {}
         g_tiles = {}
@@ -115,19 +113,21 @@ def tile_probprotoseghead_t_kernel(tc, x, x_var, prototypes, proto_var, out):
         def grouped_pairs(g, half):
             return g[:, half * 1024:(half + 1) * 1024].rearrange("q (n u e) -> q n u e", u=2, e=2)
 
-        def bias_tile(c, route):
-            table = bs_tiles if route == "s" else bn_tiles
-            if c not in table:
-                b = small.tile([P, chunks[c][1]], F32, tag="bs" if route == "s" else "bn")
-                table[c] = b
-            return table[c]
+        def bias_tile(c):
+            if c not in bn_tiles:
+                b = small.tile([P, chunks[c][1]], F32, tag="bn")
+                bn_tiles[c] = b
+            return bn_tiles[c]
 
         def row_bias(k, tt):
             route = sum_route(k, tt)
             if route == "pe":
                 return bf_tiles[k // 2][:, k % 2:k % 2 + 1]
+            if route == "g":
+                j = k // 2
+                return gb_tiles[j // 2][:, j % 2:j % 2 + 1]
             c, t0 = pairs[k]
-            return bias_tile(c, route)[:, t0 + tt:t0 + tt + 1]
+            return bias_tile(c)[:, t0 + tt:t0 + tt + 1]
 
         def sums(k):
             c, t0 = pairs[k]
@@ -135,14 +135,42 @@ def tile_probprotoseghead_t_kernel(tc, x, x_var, prototypes, proto_var, out):
                 t = t0 + tt
                 route = sum_route(k, tt)
                 src = v_tiles[c][:, t * D:(t + 1) * D]
-                if route == "s":
-                    junk_s = junks.tile([P, D], BF16, tag="junks")
-                    nc.scalar.activation(out=junk_s[:], in_=src, func=ACT.Copy, scale=-LAMDA,
-                                         accum_out=bias_tile(c, route)[:, t:t + 1])
-                elif route == "v":
+                if route == "v":
                     junk_v = junks.tile([P, D], BF16, tag="junkv")
                     nc.vector.tensor_scalar(out=junk_v[:], in0=src, scalar1=-LAMDA, scalar2=None,
-                                            op0=ALU.mult, op1=ALU.add, accum_out=bias_tile(c, route)[:, t:t + 1])
+                                            op0=ALU.mult, op1=ALU.add, accum_out=bias_tile(c)[:, t:t + 1])
+
+        def pool_fold(j):
+            k = 2 * j + 1
+            if j >= n_quads or sum_route(k, 1) != "g":
+                return
+            c, t0 = pairs[k]
+            col0 = (t0 + 1) * D
+            v_sb = v_tiles[c]
+            if j // 2 not in gs_tiles:
+                gs = small.tile([P, 2 * FOLD_N], F32, tag="gs")
+                gs_tiles[j // 2] = gs
+            halves = []
+            for h in range(2):
+                half = pools.tile([P, P], F32, tag="half%d" % h)
+                nc.gpsimd.tensor_tensor(out=half[:], in0=v_sb[:, col0 + 2 * h * P:col0 + (2 * h + 1) * P],
+                                        in1=v_sb[:, col0 + (2 * h + 1) * P:col0 + (2 * h + 2) * P], op=ALU.add)
+                halves.append(half)
+            both = pools.tile([P, P], F32, tag="both")
+            nc.gpsimd.tensor_tensor(out=both[:], in0=halves[0][:], in1=halves[1][:], op=ALU.add)
+            i = j % 2
+            nc.gpsimd.tensor_tensor(out=gs_tiles[j // 2][:, i * FOLD_N:(i + 1) * FOLD_N], in0=both[:, 0:FOLD_N],
+                                    in1=both[:, FOLD_N:2 * FOLD_N], op=ALU.add)
+
+        def pool_reduce(i):
+            if i not in gs_tiles:
+                return
+            raw = small.tile([P, 2], F32, tag="graw")
+            nc.vector.tensor_reduce(out=raw[:], in_=gs_tiles[i][:].rearrange("p (i n) -> p i n", i=2),
+                                    axis=AX.X, op=ALU.add)
+            gb = small.tile([P, 2], F32, tag="gb")
+            nc.gpsimd.tensor_scalar(out=gb[:], in0=raw[:], scalar1=-LAMDA, scalar2=0.0, op0=ALU.mult, op1=ALU.add)
+            gb_tiles[i] = gb
 
         def fold(j):
             if sum_route(2 * j, 0) != "pe":
@@ -296,6 +324,7 @@ def tile_probprotoseghead_t_kernel(tc, x, x_var, prototypes, proto_var, out):
         assert n_pairs % 2 == 0 and LOOK % 2 == 0
         n_quads = n_pairs // 2
         last = n_pairs - 1
+        pool_fold(2)
         transpose_v(0)
         for j in range(n_quads):
             first, second = 2 * j, 2 * j + 1
@@ -328,8 +357,11 @@ def tile_probprotoseghead_t_kernel(tc, x, x_var, prototypes, proto_var, out):
             for k in (first + LOOK, second + LOOK):
                 if k < n_pairs:
                     sums(k)
+            pool_fold(j + 3)
             if j + 1 < n_quads:
                 fold_reduce(j + 1)
+                if j % 2 == 1:
+                    pool_reduce((j + 1) // 2)
             if j >= 1:
                 quantise(first)
                 finish(first - 2)

@@ -61,7 +61,7 @@ def tile_probprotoseghead_t_kernel(tc, x, x_var, prototypes, proto_var, out):
         quants = ctx.enter_context(tc.tile_pool(name="quants", bufs=4))
         small = ctx.enter_context(tc.tile_pool(name="small", bufs=8))
         junks = ctx.enter_context(tc.tile_pool(name="junks", bufs=2))
-        pools = ctx.enter_context(tc.tile_pool(name="pools", bufs=2))
+        pools = ctx.enter_context(tc.tile_pool(name="pools", bufs=1))
         psum_x = ctx.enter_context(tc.psum_pool(name="psum_x", bufs=2))
         psum_v = ctx.enter_context(tc.psum_pool(name="psum_v", bufs=3))
         psum_a = ctx.enter_context(tc.psum_pool(name="psum_a", bufs=2))
@@ -70,7 +70,8 @@ def tile_probprotoseghead_t_kernel(tc, x, x_var, prototypes, proto_var, out):
         x_tiles = {}
         v_tiles = {}
         bn_tiles = {}
-        gs_tiles = {}
+        w_tiles = {}
+        raw_tiles = {}
         gb_tiles = {}
         o_tiles = {}
         banks = {}
@@ -146,30 +147,27 @@ def tile_probprotoseghead_t_kernel(tc, x, x_var, prototypes, proto_var, out):
                 return
             c, t0 = pairs[k]
             col0 = (t0 + 1) * D
-            v_sb = v_tiles[c]
-            if j // 2 not in gs_tiles:
-                gs = small.tile([P, 2 * FOLD_N], F32, tag="gs")
-                gs_tiles[j // 2] = gs
-            halves = []
-            for h in range(2):
-                half = pools.tile([P, P], F32, tag="half%d" % h)
-                nc.gpsimd.tensor_tensor(out=half[:], in0=v_sb[:, col0 + 2 * h * P:col0 + (2 * h + 1) * P],
-                                        in1=v_sb[:, col0 + (2 * h + 1) * P:col0 + (2 * h + 2) * P], op=ALU.add)
-                halves.append(half)
-            both = pools.tile([P, P], F32, tag="both")
-            nc.gpsimd.tensor_tensor(out=both[:], in0=halves[0][:], in1=halves[1][:], op=ALU.add)
-            i = j % 2
-            nc.gpsimd.tensor_tensor(out=gs_tiles[j // 2][:, i * FOLD_N:(i + 1) * FOLD_N], in0=both[:, 0:FOLD_N],
-                                    in1=both[:, FOLD_N:2 * FOLD_N], op=ALU.add)
+            half = D // 2
+            w = pools.tile([P, half], F32, tag="w")
+            nc.gpsimd.tensor_tensor(out=w[:], in0=v_tiles[c][:, col0:col0 + half],
+                                    in1=v_tiles[c][:, col0 + half:col0 + D], op=ALU.add)
+            nc.gpsimd.tensor_tensor(out=w[:, 0:P], in0=w[:, 0:P], in1=w[:, P:half], op=ALU.add)
+            w_tiles[j] = w
 
-        def pool_reduce(i):
-            if i not in gs_tiles:
+        def pool_reduce(j):
+            if j not in w_tiles:
                 return
-            raw = small.tile([P, 2], F32, tag="graw")
-            nc.vector.tensor_reduce(out=raw[:], in_=gs_tiles[i][:].rearrange("p (i n) -> p i n", i=2),
-                                    axis=AX.X, op=ALU.add)
+            if j // 2 not in raw_tiles:
+                raw = small.tile([P, 2], F32, tag="graw")
+                raw_tiles[j // 2] = raw
+            raw = raw_tiles[j // 2]
+            nc.vector.tensor_reduce(out=raw[:, j % 2:j % 2 + 1], in_=w_tiles[j][:, 0:P], axis=AX.X, op=ALU.add)
+
+        def pool_scale(i):
+            if i not in raw_tiles:
+                return
             gb = small.tile([P, 2], F32, tag="gb")
-            nc.gpsimd.tensor_scalar(out=gb[:], in0=raw[:], scalar1=-LAMDA, scalar2=0.0, op0=ALU.mult, op1=ALU.add)
+            nc.gpsimd.tensor_scalar(out=gb[:], in0=raw_tiles[i][:], scalar1=-LAMDA, scalar2=0.0, op0=ALU.mult, op1=ALU.add)
             gb_tiles[i] = gb
 
         def fold(j):
@@ -324,7 +322,6 @@ def tile_probprotoseghead_t_kernel(tc, x, x_var, prototypes, proto_var, out):
         assert n_pairs % 2 == 0 and LOOK % 2 == 0
         n_quads = n_pairs // 2
         last = n_pairs - 1
-        pool_fold(2)
         transpose_v(0)
         for j in range(n_quads):
             first, second = 2 * j, 2 * j + 1
@@ -357,13 +354,15 @@ def tile_probprotoseghead_t_kernel(tc, x, x_var, prototypes, proto_var, out):
             for k in (first + LOOK, second + LOOK):
                 if k < n_pairs:
                     sums(k)
-            pool_fold(j + 3)
             if j + 1 < n_quads:
                 fold_reduce(j + 1)
-                if j % 2 == 1:
-                    pool_reduce((j + 1) // 2)
             if j >= 1:
                 quantise(first)
+            pool_reduce(j + 1)
+            pool_fold(j + 2)
+            if j % 2 == 0:
+                pool_scale(j // 2)
+            if j >= 1:
                 finish(first - 2)
                 finish(first - 1)
         multiply(last - 1)

@@ -174,13 +174,14 @@ def tile_probprotoseghead_t_kernel(tc, x, x_var, prototypes, proto_var, out):
             if sum_route(2 * j, 0) != "pe":
                 return
             ft = psum_f.tile([P, 2 * FOLD_N], F32, tag="fold")
+            c, t0 = pairs[2 * j]
+            assert pairs[2 * j + 1] == (c, t0 + 2)
             n_folds = D // FOLD_N
-            for i in range(2):
-                c, t0 = pairs[2 * j + i]
-                for f in range(n_folds):
-                    nc.tensor.matmul(out=ft[:, i * FOLD_N:(i + 1) * FOLD_N], lhsT=negl[:],
-                                     rhs=v_tiles[c][:, t0 * D + f * FOLD_N:t0 * D + (f + 1) * FOLD_N],
-                                     start=(f == 0), stop=(f == n_folds - 1))
+            rows = v_tiles[c][:, t0 * D:(t0 + 4) * D].rearrange("p (i w) -> p i w", i=2)
+            for f in range(n_folds):
+                nc.tensor.matmul(out=ft[:].rearrange("p (i n) -> p i n", i=2), lhsT=negl[:],
+                                 rhs=rows[:, :, f * FOLD_N:(f + 1) * FOLD_N],
+                                 start=(f == 0), stop=(f == n_folds - 1))
             fold_tiles[j] = ft
 
         def fold_reduce(j):

@@ -353,7 +353,7 @@ def tile_probprotoseghead_t_kernel(tc, x, x_var, prototypes, proto_var, out):
             else:
                 quantise(first)
             for k in (first + LOOK, second + LOOK):
-                if k < n_pairs:
+                if k < n_pairs and j >= 3:
                     sums(k)
             if j + 1 < n_quads:
                 fold_reduce(j + 1)
@@ -366,6 +366,9 @@ def tile_probprotoseghead_t_kernel(tc, x, x_var, prototypes, proto_var, out):
             if j >= 1:
                 finish(first - 2)
                 finish(first - 1)
+            if j < 3:
+                sums(first + LOOK)
+                sums(second + LOOK)
         multiply(last - 1)
         quantise(last, 0, 1024)
         quantise(last, 1024, 1536)

@@ -167,7 +167,7 @@ def tile_probprotoseghead_t_kernel(tc, x, x_var, prototypes, proto_var, out):
             if i not in raw_tiles:
                 return
             gb = small.tile([P, 2], F32, tag="gb")
-            nc.gpsimd.tensor_scalar(out=gb[:], in0=raw_tiles[i][:], scalar1=-LAMDA, scalar2=0.0, op0=ALU.mult, op1=ALU.add)
+            nc.scalar.activation(out=gb[:], in_=raw_tiles[i][:], func=ACT.Copy, scale=-LAMDA)
             gb_tiles[i] = gb
 
         def fold(j):
@@ -340,6 +340,8 @@ def tile_probprotoseghead_t_kernel(tc, x, x_var, prototypes, proto_var, out):
             if j + 1 < n_quads:
                 fold(j + 1)
             evacuate(first)
+            if j % 2 == 1:
+                pool_scale(j // 2)
             if second < last:
                 evacuate(second)
             else:
@@ -361,8 +363,6 @@ def tile_probprotoseghead_t_kernel(tc, x, x_var, prototypes, proto_var, out):
                 quantise(first)
             pool_reduce(j + 1)
             pool_fold(j + 2)
-            if j % 2 == 0:
-                pool_scale(j // 2)
             if j >= 1:
                 finish(first - 2)
                 finish(first - 1)

from contextlib import ExitStack

import concourse.mybir as mybir
from concourse.masks import make_identity

F32 = mybir.dt.float32
BF16 = mybir.dt.bfloat16
U32 = mybir.dt.uint32
U8 = mybir.dt.uint8
FP8X4 = mybir.dt.float8_e4m3fn_x4
ALU = mybir.AluOpType
AX = mybir.AxisListType
ACT = mybir.ActivationFunctionType

P = 128
D = 512
N_ROWS = 12288
CM = 256
LAMDA = 1.0 / D
FLOPS = 2 * 2 * N_ROWS * D * CM

CHUNK_TILES = [2, 2, 4, 4] + [8] * 9 + [4, 4, 2, 2]
PREFETCH = 5
PINNED = True
LOOK = 4
FOLD_N = 64


def sum_route(k, tt):
    if tt == 0 and 2 <= k // 2 <= 22 and k // 2 not in (9, 16):
        return "pe"
    if tt == 1 and k % 2 == 1 and k // 2 >= 2:
        return "g"
    return "v"


def tile_probprotoseghead_t_kernel(tc, x, x_var, prototypes, proto_var, out):
    nc = tc.nc
    out2 = out.rearrange("n c m -> n (c m)")
    p2 = prototypes.rearrange("c m d -> (c m) d")
    pv2 = proto_var.rearrange("c m d -> (c m) d")

    chunks = []
    row0 = 0
    for tiles in CHUNK_TILES:
        chunks.append((row0, tiles))
        row0 += tiles * P
    assert row0 == N_ROWS
    pairs = []
    for c, (r0, tiles) in enumerate(chunks):
        for t0 in range(0, tiles, 2):
            pairs.append((c, t0))
    n_pairs = len(pairs)
    n_chunks = len(chunks)

    with ExitStack() as ctx:
        consts = ctx.enter_context(tc.tile_pool(name="consts", bufs=1))
        loads = ctx.enter_context(tc.tile_pool(name="loads", bufs=PREFETCH + 1))
        stores = ctx.enter_context(tc.tile_pool(name="stores", bufs=6))
        groups = ctx.enter_context(tc.tile_pool(name="groups", bufs=4))
        quants = ctx.enter_context(tc.tile_pool(name="quants", bufs=4))
        small = ctx.enter_context(tc.tile_pool(name="small", bufs=8))
        junks = ctx.enter_context(tc.tile_pool(name="junks", bufs=2))
        pools = ctx.enter_context(tc.tile_pool(name="pools", bufs=1))
        psum_x = ctx.enter_context(tc.psum_pool(name="psum_x", bufs=2))
        psum_v = ctx.enter_context(tc.psum_pool(name="psum_v", bufs=3))
        psum_a = ctx.enter_context(tc.psum_pool(name="psum_a", bufs=2))
        psum_f = ctx.enter_context(tc.psum_pool(name="psum_f", bufs=1))

        x_tiles = {}
        v_tiles = {}
        bn_tiles = {}
        w_tiles = {}
        raw_tiles = {}
        gb_tiles = {}
        o_tiles = {}
        banks = {}
        g_tiles = {}
        q_tiles = {}
        acc_tiles = {}
        fold_tiles = {}
        bf_tiles = {}

        ident = consts.tile([P, P], F32)
        make_identity(nc, ident[:])
        ones = consts.tile([P, P], F32)
        nc.vector.memset(ones[:], 1.0)
        negl = consts.tile([P, P], BF16)
        nc.vector.tensor_scalar(out=negl[:], in0=ident[:], scalar1=-LAMDA, scalar2=None, op0=ALU.mult)
        if PINNED:
            ctx.enter_context(tc.manual_schedule())

        def load(c):
            r0, tiles = chunks[c]
            x_sb = loads.tile([P, tiles * D], BF16, tag="x")
            v_sb = loads.tile([P, tiles * D], BF16, tag="v")
            nc.sync.dma_start(out=v_sb[:], in_=x_var[r0:r0 + tiles * P, :].rearrange("(p t) d -> p (t d)", t=tiles))
            nc.sync.dma_start(out=x_sb[:], in_=x[r0:r0 + tiles * P, :].rearrange("(p t) d -> p (t d)", t=tiles))
            x_tiles[c] = x_sb
            v_tiles[c] = v_sb

        def transpose_pair(bank, words, col0):
            for u in range(2):
                for tt in range(2):
                    nc.tensor.transpose(
                        bank[:, u * 256 + tt * P:u * 256 + (tt + 1) * P],
                        words[:, col0 + tt * 256 + u * P:col0 + tt * 256 + (u + 1) * P],
                        ident[:],
                    )

        def bf16_pairs(bank):
            return bank[:].bitcast(BF16).rearrange("q (u n e) -> q n u e", u=2, e=2)

        def grouped_pairs(g, half):
            return g[:, half * 1024:(half + 1) * 1024].rearrange("q (n u e) -> q n u e", u=2, e=2)

        def bias_tile(c):
            if c not in bn_tiles:
                b = small.tile([P, chunks[c][1]], F32, tag="bn")
                bn_tiles[c] = b
            return bn_tiles[c]

        def row_bias(k, tt):
            route = sum_route(k, tt)
            if route == "pe":
                return bf_tiles[k // 2][:, k % 2:k % 2 + 1]
            if route == "g":
                j = k // 2
                return gb_tiles[j // 2][:, j % 2:j % 2 + 1]
            c, t0 = pairs[k]
            return bias_tile(c)[:, t0 + tt:t0 + tt + 1]

        def sums(k):
            c, t0 = pairs[k]
            for tt in range(2):
                t = t0 + tt
                route = sum_route(k, tt)
                src = v_tiles[c][:, t * D:(t + 1) * D]
                if route == "v":
                    junk_v = junks.tile([P, D], BF16, tag="junkv")
                    nc.vector.tensor_scalar(out=junk_v[:], in0=src, scalar1=-LAMDA, scalar2=None,
                                            op0=ALU.mult, op1=ALU.add, accum_out=bias_tile(c)[:, t:t + 1])

        def pool_fold(j):
            k = 2 * j + 1
            if j >= n_quads or sum_route(k, 1) != "g":
                return
            c, t0 = pairs[k]
            col0 = (t0 + 1) * D
            half = D // 2
            w = pools.tile([P, half], F32, tag="w")
            nc.gpsimd.tensor_tensor(out=w[:], in0=v_tiles[c][:, col0:col0 + half],
                                    in1=v_tiles[c][:, col0 + half:col0 + D], op=ALU.add)
            nc.gpsimd.tensor_tensor(out=w[:, 0:P], in0=w[:, 0:P], in1=w[:, P:half], op=ALU.add)
            w_tiles[j] = w

        def pool_reduce(j):
            if j not in w_tiles:
                return
            if j // 2 not in raw_tiles:
                raw = small.tile([P, 2], F32, tag="graw")
                raw_tiles[j // 2] = raw
            raw = raw_tiles[j // 2]
            nc.vector.tensor_reduce(out=raw[:, j % 2:j % 2 + 1], in_=w_tiles[j][:, 0:P], axis=AX.X, op=ALU.add)

        def pool_scale(i):
            if i not in raw_tiles:
                return
            gb = small.tile([P, 2], F32, tag="gb")
            nc.scalar.activation(out=gb[:], in_=raw_tiles[i][:], func=ACT.Copy, scale=-LAMDA)
            gb_tiles[i] = gb

        def fold(j):
            if sum_route(2 * j, 0) != "pe":
                return
            ft = psum_f.tile([P, 2 * FOLD_N], F32, tag="fold")
            c, t0 = pairs[2 * j]
            assert pairs[2 * j + 1] == (c, t0 + 2)
            n_folds = D // FOLD_N
            rows = v_tiles[c][:, t0 * D:(t0 + 4) * D].rearrange("p (i w) -> p i w", i=2)
            for f in range(n_folds):
                nc.tensor.matmul(out=ft[:].rearrange("p (i n) -> p i n", i=2), lhsT=negl[:],
                                 rhs=rows[:, :, f * FOLD_N:(f + 1) * FOLD_N],
                                 start=(f == 0), stop=(f == n_folds - 1))
            fold_tiles[j] = ft

        def fold_reduce(j):
            if sum_route(2 * j, 0) != "pe":
                return
            bf = small.tile([P, 2], F32, tag="bf")
            nc.vector.tensor_reduce(out=bf[:], in_=fold_tiles[j][:].rearrange("p (i n) -> p i n", i=2),
                                    axis=AX.X, op=ALU.add)
            bf_tiles[j] = bf

        def transpose_v(k):
            c, t0 = pairs[k]
            tv = psum_v.tile([P, 512], F32, tag="tv")
            transpose_pair(tv, v_tiles[c][:].bitcast(F32), t0 * 256)
            banks[("v", k)] = tv

        def transpose_x(k):
            c, t0 = pairs[k]
            tx = psum_x.tile([P, 512], F32, tag="tx")
            transpose_pair(tx, x_tiles[c][:].bitcast(F32), t0 * 256)
            banks[("x", k)] = tx

        def group_tile(k):
            if k not in g_tiles:
                g = groups.tile([P, 2048], BF16, tag="g", align_bytes=64)
                g_tiles[k] = g
            return g_tiles[k]

        def copy_x(k):
            nc.scalar.copy(out=group_tile(k)[:, 0:1024].bitcast(F32).rearrange("q (n u) -> q n u", u=2),
                           in_=banks[("x", k)][:].rearrange("q (u n) -> q n u", u=2))

        def root_v(k, n0, n1):
            nc.scalar.activation(out=grouped_pairs(group_tile(k), 1)[:, n0:n1], in_=bf16_pairs(banks[("v", k)])[:, n0:n1],
                                 func=ACT.Sqrt)

        def evacuate(k):
            root_v(k, 0, 2 * P)
            copy_x(k)

        def quantise(k, col0=0, col1=2048):
            if k not in q_tiles:
                codes = quants.tile([P, 512], U32, tag="codes", align_bytes=64)
                scl = quants.tile([P, 512], U8, tag="scl", align_bytes=64)
                q_tiles[k] = (codes, scl)
            codes, scl = q_tiles[k]
            nc.vector.quantize_mx(out=codes[:, col0 // 4:col1 // 4].bitcast(FP8X4), scales=scl[:, col0 // 4:col1 // 4],
                                  in_=g_tiles[k][:, col0:col1])

        def multiply_tile(k, tt):
            codes, scl = q_tiles[k]
            if k not in acc_tiles:
                acc = psum_a.tile([P, 2 * CM], F32, tag="acc")
                acc_tiles[k] = acc
            for half in range(2):
                cols = slice(half * 256 + tt * P, half * 256 + (tt + 1) * P)
                pcols = slice(half * CM, (half + 1) * CM)
                nc.tensor.matmul_mx(
                    out=acc_tiles[k][:, tt * CM:(tt + 1) * CM],
                    lhsT=codes[:, cols].bitcast(FP8X4),
                    lhsT_scale=scl[:, cols],
                    rhs=pcodes[:, pcols].bitcast(FP8X4),
                    rhs_scale=pscl[:, pcols],
                    start=(half == 0),
                    stop=(half == 1),
                )

        def multiply(k):
            for tt in range(2):
                multiply_tile(k, tt)

        def finish_tile(k, tt):
            c, t0 = pairs[k]
            if c not in o_tiles:
                o_sb = stores.tile([P, chunks[c][1] * CM], F32, tag="o")
                o_tiles[c] = o_sb
            t = t0 + tt
            nc.vector.scalar_tensor_tensor(
                out=o_tiles[c][:, t * CM:(t + 1) * CM], in0=acc_tiles[k][:, tt * CM:(tt + 1) * CM],
                scalar=row_bias(k, tt), in1=bcm[:], op0=ALU.add, op1=ALU.add)

        def finish(k):
            c, t0 = pairs[k]
            r0, tiles = chunks[c]
            for tt in range(2):
                finish_tile(k, tt)
            if t0 + 2 == tiles:
                queue = nc.sync
                queue.dma_start(out=out2[r0:r0 + tiles * P, :].rearrange("(p t) m -> p (t m)", t=tiles),
                                in_=o_tiles[c][:])

        def store_tile(k, tt):
            c, t0 = pairs[k]
            r0, tiles = chunks[c]
            t = t0 + tt
            nc.sync.dma_start(out=out2[r0:r0 + tiles * P, :].rearrange("(p t) m -> p t m", t=tiles)[:, t, :],
                              in_=o_tiles[c][:, t * CM:(t + 1) * CM])

        warm = consts.tile([P, 1], F32)
        nc.scalar.activation(out=warm[:], in_=ones[:, 0:1], func=ACT.Sqrt)
        p_sb = consts.tile([P, 2 * D], BF16)
        pv_sb = consts.tile([P, 2 * D], BF16)
        nc.sync.dma_start(out=pv_sb[:].rearrange("p (h d) -> p h d", h=2), in_=pv2.rearrange("(h p) d -> p h d", p=P))
        nc.sync.dma_start(out=p_sb[:].rearrange("p (h d) -> p h d", h=2), in_=p2.rearrange("(h p) d -> p h d", p=P))
        for c in range(PREFETCH):
            load(c)

        tpv = psum_v.tile([P, 512], F32, tag="tv")
        transpose_pair(tpv, pv_sb[:].bitcast(F32), 0)
        tp = psum_x.tile([P, 512], F32, tag="tx")
        transpose_pair(tp, p_sb[:].bitcast(F32), 0)
        pg = consts.tile([P, 2048], BF16, align_bytes=64)
        nc.scalar.activation(out=grouped_pairs(pg, 1), in_=bf16_pairs(tpv), func=ACT.Sqrt, scale=2.0 ** -16)
        spn = consts.tile([P, 2], F32)
        rep = consts.tile([P, 2 * P], F32)
        for h in range(2):
            junk = junks.tile([P, D], BF16, tag="junkv")
            nc.vector.tensor_scalar(out=junk[:], in0=pv_sb[:, h * D:(h + 1) * D], scalar1=-LAMDA, scalar2=None,
                                    op0=ALU.mult, op1=ALU.add, accum_out=spn[:, h:h + 1])
        for h in range(2):
            nc.vector.tensor_scalar(out=rep[:, h * P:(h + 1) * P], in0=ones[:], scalar1=spn[:, h:h + 1], scalar2=-2.0,
                                    op0=ALU.mult, op1=ALU.add)
        nc.vector.tensor_scalar(out=grouped_pairs(pg, 0), in0=bf16_pairs(tp), scalar1=2.0, scalar2=None, op0=ALU.mult)
        for k in range(min(2, LOOK)):
            sums(k)
        pcodes = consts.tile([P, 512], U32, align_bytes=64)
        pscl = consts.tile([P, 512], U8, align_bytes=64)
        nc.vector.quantize_mx(out=pcodes[:].bitcast(FP8X4), scales=pscl[:], in_=pg[:])
        for k in range(min(2, LOOK), LOOK):
            sums(k)
        bcm = consts.tile([P, CM], F32)

        def spread_prototype_sums():
            bb = psum_a.tile([P, CM], F32, tag="acc")
            for h in range(2):
                nc.tensor.transpose(bb[:, h * P:(h + 1) * P], rep[:, h * P:(h + 1) * P], ident[:])
            nc.vector.tensor_copy(out=bcm[:], in_=bb[:])

        assert n_pairs % 2 == 0 and LOOK % 2 == 0
        n_quads = n_pairs // 2
        last = n_pairs - 1
        transpose_v(0)
        for j in range(n_quads):
            first, second = 2 * j, 2 * j + 1
            transpose_x(first)
            transpose_v(second)
            if second < last:
                transpose_v(second + 1)
            transpose_x(second)
            for k in (first, second):
                c, t0 = pairs[k]
                if t0 == 0 and c + PREFETCH < n_chunks:
                    load(c + PREFETCH)
            if j == 0:
                spread_prototype_sums()
            if j + 1 < n_quads:
                fold(j + 1)
            evacuate(first)
            if j % 2 == 1:
                pool_scale(j // 2)
            if second < last:
                evacuate(second)
            else:
                copy_x(last)
                root_v(last, 0, P)
                root_v(last, P, 2 * P)
            if j >= 1:
                quantise(first - 1)
                multiply(first - 2)
                multiply(first - 1)
            else:
                quantise(first)
            for k in (first + LOOK, second + LOOK):
                if k < n_pairs and j >= 3:
                    sums(k)
            if j + 1 < n_quads:
                fold_reduce(j + 1)
            if j >= 1:
                quantise(first)
            pool_reduce(j + 1)
            pool_fold(j + 2)
            if j >= 1:
                finish(first - 2)
                finish(first - 1)
            if j < 3:
                sums(first + LOOK)
                sums(second + LOOK)
        multiply(last - 1)
        quantise(last, 0, 1024)
        quantise(last, 1024, 1536)
        multiply_tile(last, 0)
        quantise(last, 1536, 2048)
        multiply_tile(last, 1)
        finish(last - 1)
        for tt in range(2):
            finish_tile(last, tt)
            store_tile(last, tt)
